import numpy as np
import ml_dtypes


def mxq(x, axis, fmt="e4m3"):
    dtype, down = {"e4m3": (ml_dtypes.float8_e4m3fn, 7), "e5m2": (ml_dtypes.float8_e5m2, 14)}[fmt]
    v = np.moveaxis(np.asarray(x, np.float32).astype(ml_dtypes.bfloat16).astype(np.float64), axis, -1)
    blocks = v.reshape(v.shape[:-1] + (-1, 32))
    amax = np.abs(blocks).max(-1, keepdims=True)
    byte = np.maximum(np.where(amax > 0, np.frexp(amax)[1] - 1 + 127, 0) - down, 1)
    scale = np.exp2(byte - 127.0)
    codes = (blocks / scale).astype(np.float32).astype(dtype).astype(np.float64)
    return np.moveaxis((codes * scale).reshape(v.shape), -1, axis)


WIDE = False


def mx_kscale(k):
    if not WIDE:
        return np.ones(k)
    levels = np.array([10, -10, 5, -5, 0])
    a = np.random.permutation(np.resize(levels, k // 512 * 4)).reshape(k // 512, 4)
    idx = np.arange(k)
    return np.exp2(a[idx // 512, idx % 128 // 32])


BF16 = ml_dtypes.bfloat16


def bf(x):
    return np.asarray(x, np.float32).astype(BF16)


def f64(x):
    return np.asarray(x).astype(np.float64)


E2M1 = np.array([0.0, 0.5, 1.0, 1.5, 2.0, 3.0, 4.0, 6.0, -0.0, -0.5, -1.0, -1.5, -2.0, -3.0, -4.0, -6.0])


def pack_weight(w, fmt):
    k, n = w.shape
    w = f64(bf(w)).reshape(k // 32, 32, n)
    amax = np.abs(w).max(1)
    if fmt == "e4m3":
        byte = np.frexp(amax)[1] - 1 + 127 - 7
    else:
        mant, ex = np.frexp(amax / 6.0)
        byte = np.where(mant > 0.5, ex, ex - 1) + 127
    byte = np.clip(np.where(amax > 0, byte, 1), 1, 254)
    scaled = (w * np.exp2(127.0 - byte)[:, None, :]).reshape(k, n).astype(np.float32)
    by_word = np.ascontiguousarray(scaled.reshape(k // 512, 128, 4, n).transpose(0, 1, 3, 2))
    if fmt == "e4m3":
        words = by_word.astype(ml_dtypes.float8_e4m3fn).view(np.uint8)
    else:
        c = by_word.astype(ml_dtypes.float4_e2m1fn).view(np.uint8) & 0xF
        words = c[..., 0::2] | (c[..., 1::2] << 4)
    return np.ascontiguousarray(words), np.ascontiguousarray(byte.astype(np.uint8).reshape(k // 512, 16, n))


def unpack_weight(words, scales, fmt):
    g, p, n, _ = words.shape
    if fmt == "e4m3":
        vals = np.ascontiguousarray(words).view(ml_dtypes.float8_e4m3fn).astype(np.float64)
    else:
        nib = np.empty((g, p, n, 4), np.uint8)
        nib[..., 0::2] = words & 0xF
        nib[..., 1::2] = words >> 4
        vals = E2M1[nib]
    vals = vals * np.repeat(np.exp2(scales.astype(np.float64) - 127.0), 8, axis=1)[..., None]
    return vals.transpose(0, 1, 3, 2).reshape(g * 512, n)


B, T, H, DK, DH, E, V = 4, 1024, 8, 64, 64, 1024, 1536
HK = H * DK
FMT = "e4m3"


def rotate_every_two(u):
    u1 = u[..., ::2]
    u2 = u[..., 1::2]
    return np.stack((-u2, u1), axis=-1).reshape(u.shape)


def theta_shift(u, sin, cos):
    return u * cos + rotate_every_two(u) * sin


def setup_inputs():
    s = mx_kscale(E)
    x = bf(np.random.standard_normal((B, T, E)) * s)
    sin = bf(np.random.standard_normal((T, DK)) * 0.7)
    cos = bf(np.random.standard_normal((T, DK)) * 0.7)
    Wq_words, Wq_scales = pack_weight(np.random.standard_normal((E, HK)) / np.sqrt(E) / s[:, None], FMT)
    Wk_words, Wk_scales = pack_weight(np.random.standard_normal((E, HK)) / np.sqrt(E) / s[:, None], FMT)
    return {"x": x,
            "sin": sin,
            "cos": cos,
            "Wq_words": Wq_words,
            "Wq_scales": Wq_scales,
            "Wk_words": Wk_words,
            "Wk_scales": Wk_scales}


def reference(x, sin, cos, Wq_words, Wq_scales, Wk_words, Wk_scales):
    xq = mxq(f64(x), 2, "e4m3")
    q = (xq @ unpack_weight(Wq_words, Wq_scales, FMT)).reshape(B, T, H, DK).transpose(0, 2, 1, 3)
    k = (xq @ unpack_weight(Wk_words, Wk_scales, FMT)).reshape(B, T, H, DK).transpose(0, 2, 1, 3)
    qr = theta_shift(q, f64(sin), f64(cos))
    kr = theta_shift(k, f64(sin), f64(cos))
    return qr, kr

@@ -1,0 +1,161 @@
+from contextlib import ExitStack
+
+import concourse.mybir as mybir
+from concourse.masks import make_identity
+
+F32 = mybir.dt.float32
+BF16 = mybir.dt.bfloat16
+I32 = mybir.dt.int32
+U32 = mybir.dt.uint32
+U8 = mybir.dt.uint8
+FP8X4 = mybir.dt.float8_e4m3fn_x4
+
+B, T, H, DK, E = 4, 1024, 8, 64, 1024
+HK = H * DK
+PAIRS = DK // 2
+
+P = 128
+PACK = 4
+K_PASS = P * PACK
+PASSES = E // K_PASS
+WORDS = K_PASS // 2
+
+ROWS = 4
+GROUP = P * ROWS
+GROUPS_PER_SEQ = T // GROUP
+N_GROUPS = B * GROUPS_PER_SEQ
+
+FLOPS = 2 * B * T * E * 2 * HK
+
+
+def tile_multiscaleretention_pa_t_kernel(
+    tc, x, sin, cos, Wq_words, Wq_scales, Wk_words, Wk_scales, out_0, out_1
+):
+    nc = tc.nc
+    weights = ((Wq_words, Wq_scales), (Wk_words, Wk_scales))
+    outs = (out_0, out_1)
+    x_groups = x.rearrange("b (s p j) e -> (b s) p j e", p=P, j=ROWS)
+
+    with ExitStack() as ctx:
+        const = ctx.enter_context(tc.tile_pool(name="const", bufs=1))
+        x_pool = ctx.enter_context(tc.tile_pool(name="x", bufs=N_GROUPS))
+        grouped_pool = ctx.enter_context(tc.tile_pool(name="grouped", bufs=2))
+        mx_pool = ctx.enter_context(tc.tile_pool(name="mx", bufs=3))
+        prod_pool = ctx.enter_context(tc.tile_pool(name="prod", bufs=3))
+        stage_pool = ctx.enter_context(tc.tile_pool(name="stage", bufs=4))
+        xt_pool = ctx.enter_context(tc.psum_pool(name="xt", bufs=ROWS))
+        acc_pool = ctx.enter_context(tc.psum_pool(name="acc", bufs=4))
+
+        ident = const.tile([P, P], F32)
+        make_identity(nc, ident[:])
+
+        w_words = const.tile([P, 2, PASSES, HK], U32, align_bytes=64)
+        w_planes = const.tile([P, 2, PASSES, HK], U8, align_bytes=64)
+        nc.vector.memset(w_planes[:].bitcast(I32), 0)
+
+        def load_x(n):
+            x_sb = x_pool.tile([P, ROWS, E], BF16)
+            for j in range(ROWS):
+                nc.sync.dma_start(out=x_sb[:, j, :], in_=x_groups[n][:, j, :])
+            return x_sb
+
+        def load_weight(qk):
+            words, scales = weights[qk]
+            nc.sync.dma_start(
+                out=w_words[:, qk].bitcast(I32),
+                in_=words.rearrange("g p n t -> p g (n t)").bitcast(I32),
+            )
+            by_row = scales.rearrange("g (q r) n -> r q g n", r=4)
+            for r in range(4):
+                nc.sync.dma_start(
+                    out=w_planes[r:P:32, qk].bitcast(I32), in_=by_row[r].bitcast(I32)
+                )
+
+        x_tiles = [load_x(0)]
+        load_weight(0)
+        cos_sb = const.tile([P, GROUPS_PER_SEQ, ROWS, DK], BF16)
+        sin_sb = const.tile([P, GROUPS_PER_SEQ, ROWS, DK], BF16)
+        nc.scalar.dma_start(out=cos_sb[:], in_=cos.rearrange("(s p j) c -> p s j c", p=P, j=ROWS))
+        nc.scalar.dma_start(out=sin_sb[:], in_=sin.rearrange("(s p j) c -> p s j c", p=P, j=ROWS))
+        load_weight(1)
+        for n in range(1, N_GROUPS):
+            x_tiles.append(load_x(n))
+
+        rot = const.tile([P, GROUPS_PER_SEQ, ROWS, PAIRS, 2, 2], BF16)
+        rot_v = rot[:].rearrange("p s j i e k -> p (s j) i e k")
+        cos_v = cos_sb[:].rearrange("p s j (i e) -> p (s j) i e", e=2)
+        sin_v = sin_sb[:].rearrange("p s j (i e) -> p (s j) i e", e=2)
+        nc.vector.tensor_copy(out=rot_v[:, :, :, 0, 0], in_=cos_v[:, :, :, 0])
+        nc.vector.tensor_scalar_mul(out=rot_v[:, :, :, 0, 1], in0=sin_v[:, :, :, 0], scalar1=-1.0)
+        nc.vector.tensor_copy(out=rot_v[:, :, :, 1, 0], in_=sin_v[:, :, :, 1])
+        nc.vector.tensor_copy(out=rot_v[:, :, :, 1, 1], in_=cos_v[:, :, :, 1])
+
+        def quantise_group(n):
+            x_sb = x_tiles[n]
+            grouped = grouped_pool.tile([P, ROWS, PASSES * P * PACK], BF16, align_bytes=64)
+            for j in range(ROWS):
+                x_words = x_sb[:, j, :].bitcast(F32)
+                xt = xt_pool.tile([P, PASSES, 2, P], F32)
+                for g in range(PASSES):
+                    for u in range(2):
+                        nc.tensor.transpose(
+                            xt[:, g, u, :],
+                            x_words[:, WORDS * g + u : WORDS * (g + 1) : 2],
+                            ident[:],
+                        )
+                nc.scalar.copy(
+                    out=grouped[:, j, :].bitcast(F32).rearrange("p (g r u) -> p g r u", g=PASSES, u=2),
+                    in_=xt[:].rearrange("p g u r -> p g r u"),
+                )
+            x_codes = mx_pool.tile([P, ROWS, PASSES * P], U32, align_bytes=64)
+            x_planes = mx_pool.tile([P, ROWS, PASSES * P], U8, align_bytes=64)
+            nc.vector.quantize_mx(
+                out=x_codes[:].rearrange("p j w -> p (j w)").bitcast(FP8X4),
+                scales=x_planes[:].rearrange("p j w -> p (j w)"),
+                in_=grouped[:].rearrange("p j v -> p (j v)"),
+            )
+            return x_codes, x_planes
+
+        def project_group(n, x_codes, x_planes):
+            b, s = divmod(n, GROUPS_PER_SEQ)
+            for qk in range(2):
+                stage = stage_pool.tile([P, H, ROWS, DK], F32)
+                for j0 in range(0, ROWS, 2):
+                    prod = prod_pool.tile([P, 2, H, PAIRS, 2, 2], F32)
+                    for j in (j0, j0 + 1):
+                        acc = acc_pool.tile([P, HK], F32)
+                        for g in range(PASSES):
+                            tokens = slice(g * P, (g + 1) * P)
+                            nc.tensor.matmul_mx(
+                                out=acc[:],
+                                lhsT=x_codes[:, j, tokens].bitcast(FP8X4),
+                                lhsT_scale=x_planes[:, j, tokens],
+                                rhs=w_words[:, qk, g, :].bitcast(FP8X4),
+                                rhs_scale=w_planes[:, qk, g, :],
+                                start=(g == 0),
+                                stop=(g == PASSES - 1),
+                            )
+                        shape = [P, H, PAIRS, 2, 2]
+                        nc.vector.tensor_tensor(
+                            out=prod[:, j - j0],
+                            in0=acc[:].rearrange("p (h i k) -> p h i k", h=H, k=2).unsqueeze(3).to_broadcast(shape),
+                            in1=rot[:, s, j].unsqueeze(1).to_broadcast(shape),
+                            op=mybir.AluOpType.mult,
+                        )
+                    terms = prod[:].rearrange("p j h i e k -> p j h (i e) k")
+                    nc.gpsimd.tensor_tensor(
+                        out=stage[:, :, j0 : j0 + 2, :].rearrange("p h j c -> p j h c"),
+                        in0=terms[:, :, :, :, 0],
+                        in1=terms[:, :, :, :, 1],
+                        op=mybir.AluOpType.add,
+                    )
+                nc.sync.dma_start(
+                    out=outs[qk][b].rearrange("h (s p j) c -> s p h (j c)", p=P, j=ROWS)[s],
+                    in_=stage[:].rearrange("p h j c -> p h (j c)"),
+                )
+
+        ready = quantise_group(0)
+        for n in range(N_GROUPS):
+            following = quantise_group(n + 1) if n + 1 < N_GROUPS else None
+            project_group(n, ready[0], ready[1])
+            ready = following

@@ -41,7 +41,7 @@ def tile_multiscaleretention_pa_t_kernel(
         x_pool = ctx.enter_context(tc.tile_pool(name="x", bufs=N_GROUPS))
         grouped_pool = ctx.enter_context(tc.tile_pool(name="grouped", bufs=2))
         mx_pool = ctx.enter_context(tc.tile_pool(name="mx", bufs=3))
-        prod_pool = ctx.enter_context(tc.tile_pool(name="prod", bufs=3))
+        prod_pool = ctx.enter_context(tc.tile_pool(name="prod", bufs=4))
         stage_pool = ctx.enter_context(tc.tile_pool(name="stage", bufs=4))
         xt_pool = ctx.enter_context(tc.psum_pool(name="xt", bufs=ROWS))
         acc_pool = ctx.enter_context(tc.psum_pool(name="acc", bufs=4))
@@ -90,9 +90,11 @@ def tile_multiscaleretention_pa_t_kernel(
         nc.vector.tensor_copy(out=rot_v[:, :, :, 1, 0], in_=sin_v[:, :, :, 1])
         nc.vector.tensor_copy(out=rot_v[:, :, :, 1, 1], in_=cos_v[:, :, :, 1])
 
-        def quantise_group(n):
+        def quantise_group(n, tiles_per_call):
             x_sb = x_tiles[n]
             grouped = grouped_pool.tile([P, ROWS, PASSES * P * PACK], BF16, align_bytes=64)
+            x_codes = mx_pool.tile([P, ROWS, PASSES * P], U32, align_bytes=64)
+            x_planes = mx_pool.tile([P, ROWS, PASSES * P], U8, align_bytes=64)
             for j in range(ROWS):
                 x_words = x_sb[:, j, :].bitcast(F32)
                 xt = xt_pool.tile([P, PASSES, 2, P], F32)
@@ -107,13 +109,13 @@ def tile_multiscaleretention_pa_t_kernel(
                     out=grouped[:, j, :].bitcast(F32).rearrange("p (g r u) -> p g r u", g=PASSES, u=2),
                     in_=xt[:].rearrange("p g u r -> p g r u"),
                 )
-            x_codes = mx_pool.tile([P, ROWS, PASSES * P], U32, align_bytes=64)
-            x_planes = mx_pool.tile([P, ROWS, PASSES * P], U8, align_bytes=64)
-            nc.vector.quantize_mx(
-                out=x_codes[:].rearrange("p j w -> p (j w)").bitcast(FP8X4),
-                scales=x_planes[:].rearrange("p j w -> p (j w)"),
-                in_=grouped[:].rearrange("p j v -> p (j v)"),
-            )
+                if (j + 1) % tiles_per_call == 0:
+                    tiles = slice(j + 1 - tiles_per_call, j + 1)
+                    nc.vector.quantize_mx(
+                        out=x_codes[:, tiles, :].rearrange("p j w -> p (j w)").bitcast(FP8X4),
+                        scales=x_planes[:, tiles, :].rearrange("p j w -> p (j w)"),
+                        in_=grouped[:, tiles, :].rearrange("p j v -> p (j v)"),
+                    )
             return x_codes, x_planes
 
         def project_group(n, x_codes, x_planes):
@@ -154,8 +156,8 @@ def tile_multiscaleretention_pa_t_kernel(
                     in_=stage[:].rearrange("p h j c -> p h (j c)"),
                 )
 
-        ready = quantise_group(0)
+        ready = quantise_group(0, 1)
         for n in range(N_GROUPS):
-            following = quantise_group(n + 1) if n + 1 < N_GROUPS else None
+            following = quantise_group(n + 1, ROWS) if n + 1 < N_GROUPS else None
             project_group(n, ready[0], ready[1])
             ready = following

@@ -20,9 +20,8 @@ K_PASS = P * PACK
 PASSES = E // K_PASS
 WORDS = K_PASS // 2
 
-ROWS = 4
-GROUP = P * ROWS
-GROUPS_PER_SEQ = T // GROUP
+ROWS = 2
+GROUPS_PER_SEQ = T // (P * ROWS)
 N_GROUPS = B * GROUPS_PER_SEQ
 
 FLOPS = 2 * B * T * E * 2 * HK
@@ -42,22 +41,24 @@ def tile_multiscaleretention_pa_t_kernel(
         grouped_pool = ctx.enter_context(tc.tile_pool(name="grouped", bufs=2))
         mx_pool = ctx.enter_context(tc.tile_pool(name="mx", bufs=3))
         prod_pool = ctx.enter_context(tc.tile_pool(name="prod", bufs=4))
-        stage_pool = ctx.enter_context(tc.tile_pool(name="stage", bufs=4))
+        stage_pool = ctx.enter_context(tc.tile_pool(name="stage", bufs=6))
         xt_pool = ctx.enter_context(tc.psum_pool(name="xt", bufs=ROWS))
-        acc_pool = ctx.enter_context(tc.psum_pool(name="acc", bufs=4))
+        acc_pool = ctx.enter_context(tc.psum_pool(name="acc", bufs=8 - ROWS))
 
-        ident = const.tile([P, P], F32)
-        make_identity(nc, ident[:])
+        cos_sb = const.tile([P, GROUPS_PER_SEQ, ROWS, DK], BF16)
+        sin_sb = const.tile([P, GROUPS_PER_SEQ, ROWS, DK], BF16)
+        nc.scalar.dma_start(out=cos_sb[:], in_=cos.rearrange("(s p j) c -> p s j c", p=P, j=ROWS))
+        nc.scalar.dma_start(out=sin_sb[:], in_=sin.rearrange("(s p j) c -> p s j c", p=P, j=ROWS))
 
         w_words = const.tile([P, 2, PASSES, HK], U32, align_bytes=64)
         w_planes = const.tile([P, 2, PASSES, HK], U8, align_bytes=64)
         nc.vector.memset(w_planes[:].bitcast(I32), 0)
 
+        x_tiles = [x_pool.tile([P, ROWS, E], BF16, name="x_sb") for n in range(N_GROUPS)]
+
         def load_x(n):
-            x_sb = x_pool.tile([P, ROWS, E], BF16)
             for j in range(ROWS):
-                nc.sync.dma_start(out=x_sb[:, j, :], in_=x_groups[n][:, j, :])
-            return x_sb
+                nc.sync.dma_start(out=x_tiles[n][:, j, :], in_=x_groups[n][:, j, :])
 
         def load_weight(qk):
             words, scales = weights[qk]
@@ -71,15 +72,15 @@ def tile_multiscaleretention_pa_t_kernel(
                     out=w_planes[r:P:32, qk].bitcast(I32), in_=by_row[r].bitcast(I32)
                 )
 
-        x_tiles = [load_x(0)]
+        load_x(0)
         load_weight(0)
-        cos_sb = const.tile([P, GROUPS_PER_SEQ, ROWS, DK], BF16)
-        sin_sb = const.tile([P, GROUPS_PER_SEQ, ROWS, DK], BF16)
-        nc.scalar.dma_start(out=cos_sb[:], in_=cos.rearrange("(s p j) c -> p s j c", p=P, j=ROWS))
-        nc.scalar.dma_start(out=sin_sb[:], in_=sin.rearrange("(s p j) c -> p s j c", p=P, j=ROWS))
+        load_x(1)
         load_weight(1)
-        for n in range(1, N_GROUPS):
-            x_tiles.append(load_x(n))
+        for n in range(2, N_GROUPS):
+            load_x(n)
+
+        ident = const.tile([P, P], F32)
+        make_identity(nc, ident[:])
 
         rot = const.tile([P, GROUPS_PER_SEQ, ROWS, PAIRS, 2, 2], BF16)
         rot_v = rot[:].rearrange("p s j i e k -> p (s j) i e k")
@@ -90,13 +91,10 @@ def tile_multiscaleretention_pa_t_kernel(
         nc.vector.tensor_copy(out=rot_v[:, :, :, 1, 0], in_=sin_v[:, :, :, 1])
         nc.vector.tensor_copy(out=rot_v[:, :, :, 1, 1], in_=cos_v[:, :, :, 1])
 
-        def quantise_group(n, tiles_per_call):
-            x_sb = x_tiles[n]
+        def quantise(n):
             grouped = grouped_pool.tile([P, ROWS, PASSES * P * PACK], BF16, align_bytes=64)
-            x_codes = mx_pool.tile([P, ROWS, PASSES * P], U32, align_bytes=64)
-            x_planes = mx_pool.tile([P, ROWS, PASSES * P], U8, align_bytes=64)
             for j in range(ROWS):
-                x_words = x_sb[:, j, :].bitcast(F32)
+                x_words = x_tiles[n][:, j, :].bitcast(F32)
                 xt = xt_pool.tile([P, PASSES, 2, P], F32)
                 for g in range(PASSES):
                     for u in range(2):
@@ -109,55 +107,54 @@ def tile_multiscaleretention_pa_t_kernel(
                     out=grouped[:, j, :].bitcast(F32).rearrange("p (g r u) -> p g r u", g=PASSES, u=2),
                     in_=xt[:].rearrange("p g u r -> p g r u"),
                 )
-                if (j + 1) % tiles_per_call == 0:
-                    tiles = slice(j + 1 - tiles_per_call, j + 1)
-                    nc.vector.quantize_mx(
-                        out=x_codes[:, tiles, :].rearrange("p j w -> p (j w)").bitcast(FP8X4),
-                        scales=x_planes[:, tiles, :].rearrange("p j w -> p (j w)"),
-                        in_=grouped[:, tiles, :].rearrange("p j v -> p (j v)"),
-                    )
+            x_codes = mx_pool.tile([P, ROWS, PASSES * P], U32, align_bytes=64)
+            x_planes = mx_pool.tile([P, ROWS, PASSES * P], U8, align_bytes=64)
+            nc.vector.quantize_mx(
+                out=x_codes[:].rearrange("p j w -> p (j w)").bitcast(FP8X4),
+                scales=x_planes[:].rearrange("p j w -> p (j w)"),
+                in_=grouped[:].rearrange("p j v -> p (j v)"),
+            )
             return x_codes, x_planes
 
-        def project_group(n, x_codes, x_planes):
+        def project(n, qk, x_codes, x_planes):
             b, s = divmod(n, GROUPS_PER_SEQ)
-            for qk in range(2):
-                stage = stage_pool.tile([P, H, ROWS, DK], F32)
-                for j0 in range(0, ROWS, 2):
-                    prod = prod_pool.tile([P, 2, H, PAIRS, 2, 2], F32)
-                    for j in (j0, j0 + 1):
-                        acc = acc_pool.tile([P, HK], F32)
-                        for g in range(PASSES):
-                            tokens = slice(g * P, (g + 1) * P)
-                            nc.tensor.matmul_mx(
-                                out=acc[:],
-                                lhsT=x_codes[:, j, tokens].bitcast(FP8X4),
-                                lhsT_scale=x_planes[:, j, tokens],
-                                rhs=w_words[:, qk, g, :].bitcast(FP8X4),
-                                rhs_scale=w_planes[:, qk, g, :],
-                                start=(g == 0),
-                                stop=(g == PASSES - 1),
-                            )
-                        shape = [P, H, PAIRS, 2, 2]
-                        nc.vector.tensor_tensor(
-                            out=prod[:, j - j0],
-                            in0=acc[:].rearrange("p (h i k) -> p h i k", h=H, k=2).unsqueeze(3).to_broadcast(shape),
-                            in1=rot[:, s, j].unsqueeze(1).to_broadcast(shape),
-                            op=mybir.AluOpType.mult,
-                        )
-                    terms = prod[:].rearrange("p j h i e k -> p j h (i e) k")
-                    nc.gpsimd.tensor_tensor(
-                        out=stage[:, :, j0 : j0 + 2, :].rearrange("p h j c -> p j h c"),
-                        in0=terms[:, :, :, :, 0],
-                        in1=terms[:, :, :, :, 1],
-                        op=mybir.AluOpType.add,
+            prod = prod_pool.tile([P, ROWS, H, PAIRS, 2, 2], F32)
+            for j in range(ROWS):
+                acc = acc_pool.tile([P, HK], F32)
+                for g in range(PASSES):
+                    tokens = slice(g * P, (g + 1) * P)
+                    nc.tensor.matmul_mx(
+                        out=acc[:],
+                        lhsT=x_codes[:, j, tokens].bitcast(FP8X4),
+                        lhsT_scale=x_planes[:, j, tokens],
+                        rhs=w_words[:, qk, g, :].bitcast(FP8X4),
+                        rhs_scale=w_planes[:, qk, g, :],
+                        start=(g == 0),
+                        stop=(g == PASSES - 1),
                     )
-                nc.sync.dma_start(
-                    out=outs[qk][b].rearrange("h (s p j) c -> s p h (j c)", p=P, j=ROWS)[s],
-                    in_=stage[:].rearrange("p h j c -> p h (j c)"),
+                shape = [P, H, PAIRS, 2, 2]
+                nc.vector.tensor_tensor(
+                    out=prod[:, j],
+                    in0=acc[:].rearrange("p (h i k) -> p h i k", h=H, k=2).unsqueeze(3).to_broadcast(shape),
+                    in1=rot[:, s, j].unsqueeze(1).to_broadcast(shape),
+                    op=mybir.AluOpType.mult,
                 )
+            stage = stage_pool.tile([P, H, ROWS, DK], F32)
+            terms = prod[:].rearrange("p j h i e k -> p j h (i e) k")
+            nc.gpsimd.tensor_tensor(
+                out=stage[:].rearrange("p h j c -> p j h c"),
+                in0=terms[:, :, :, :, 0],
+                in1=terms[:, :, :, :, 1],
+                op=mybir.AluOpType.add,
+            )
+            nc.sync.dma_start(
+                out=outs[qk][b].rearrange("h (s p j) c -> s p h (j c)", p=P, j=ROWS)[s],
+                in_=stage[:].rearrange("p h j c -> p h (j c)"),
+            )
 
-        ready = quantise_group(0, 1)
+        ready = quantise(0)
         for n in range(N_GROUPS):
-            following = quantise_group(n + 1, ROWS) if n + 1 < N_GROUPS else None
-            project_group(n, ready[0], ready[1])
+            project(n, 0, ready[0], ready[1])
+            following = quantise(n + 1) if n + 1 < N_GROUPS else None
+            project(n, 1, ready[0], ready[1])
             ready = following

@@ -9,6 +9,8 @@ I32 = mybir.dt.int32
 U32 = mybir.dt.uint32
 U8 = mybir.dt.uint8
 FP8X4 = mybir.dt.float8_e4m3fn_x4
+MULT = mybir.AluOpType.mult
+ADD = mybir.AluOpType.add
 
 B, T, H, DK, E = 4, 1024, 8, 64, 1024
 HK = H * DK
@@ -34,67 +36,83 @@ def tile_multiscaleretention_pa_t_kernel(
     weights = ((Wq_words, Wq_scales), (Wk_words, Wk_scales))
     outs = (out_0, out_1)
     x_groups = x.rearrange("b (s p j) e -> (b s) p j e", p=P, j=ROWS)
+    trig_hbm = [t.rearrange("(s p j) c -> p s j c", p=P, j=ROWS) for t in (cos, sin)]
 
     with ExitStack() as ctx:
         const = ctx.enter_context(tc.tile_pool(name="const", bufs=1))
-        x_pool = ctx.enter_context(tc.tile_pool(name="x", bufs=N_GROUPS))
+        x_pool = ctx.enter_context(tc.tile_pool(name="x", bufs=N_GROUPS * ROWS))
         grouped_pool = ctx.enter_context(tc.tile_pool(name="grouped", bufs=2))
-        mx_pool = ctx.enter_context(tc.tile_pool(name="mx", bufs=3))
-        prod_pool = ctx.enter_context(tc.tile_pool(name="prod", bufs=4))
-        stage_pool = ctx.enter_context(tc.tile_pool(name="stage", bufs=6))
+        mx_pool = ctx.enter_context(tc.tile_pool(name="mx", bufs=4))
+        prod_pool = ctx.enter_context(tc.tile_pool(name="prod", bufs=5))
+        stage_pool = ctx.enter_context(tc.tile_pool(name="stage", bufs=12))
         xt_pool = ctx.enter_context(tc.psum_pool(name="xt", bufs=ROWS))
         acc_pool = ctx.enter_context(tc.psum_pool(name="acc", bufs=8 - ROWS))
 
-        cos_sb = const.tile([P, GROUPS_PER_SEQ, ROWS, DK], BF16)
-        sin_sb = const.tile([P, GROUPS_PER_SEQ, ROWS, DK], BF16)
-        nc.scalar.dma_start(out=cos_sb[:], in_=cos.rearrange("(s p j) c -> p s j c", p=P, j=ROWS))
-        nc.scalar.dma_start(out=sin_sb[:], in_=sin.rearrange("(s p j) c -> p s j c", p=P, j=ROWS))
+        parts = (slice(0, 1), slice(1, GROUPS_PER_SEQ))
+        trig = [
+            [
+                const.tile([P, part.stop - part.start, ROWS, DK], BF16, name="trig%d%d" % (which, at))
+                for at, part in enumerate(parts)
+            ]
+            for which in range(2)
+        ]
+        for which in range(2):
+            nc.scalar.dma_start(out=trig[which][0][:], in_=trig_hbm[which][:, parts[0]])
 
-        w_words = const.tile([P, 2, PASSES, HK], U32, align_bytes=64)
-        w_planes = const.tile([P, 2, PASSES, HK], U8, align_bytes=64)
-        nc.vector.memset(w_planes[:].bitcast(I32), 0)
+        w_words = [const.tile([P, PASSES, HK], U32, align_bytes=64, name="w_words%d" % qk) for qk in range(2)]
+        w_planes = [const.tile([P, PASSES, HK], U8, align_bytes=64, name="w_planes%d" % qk) for qk in range(2)]
+        for qk in range(2):
+            nc.vector.memset(w_planes[qk][:].bitcast(I32), 0)
 
-        x_tiles = [x_pool.tile([P, ROWS, E], BF16, name="x_sb") for n in range(N_GROUPS)]
+        x_tiles = [[x_pool.tile([P, E], BF16, name="x_sb") for j in range(ROWS)] for n in range(N_GROUPS)]
 
-        def load_x(n):
-            for j in range(ROWS):
-                nc.sync.dma_start(out=x_tiles[n][:, j, :], in_=x_groups[n][:, j, :])
+        def load_x(n, j):
+            nc.sync.dma_start(out=x_tiles[n][j][:], in_=x_groups[n][:, j, :])
 
         def load_weight(qk):
             words, scales = weights[qk]
             nc.sync.dma_start(
-                out=w_words[:, qk].bitcast(I32),
+                out=w_words[qk][:].bitcast(I32),
                 in_=words.rearrange("g p n t -> p g (n t)").bitcast(I32),
             )
             by_row = scales.rearrange("g (q r) n -> r q g n", r=4)
             for r in range(4):
-                nc.sync.dma_start(
-                    out=w_planes[r:P:32, qk].bitcast(I32), in_=by_row[r].bitcast(I32)
-                )
+                nc.sync.dma_start(out=w_planes[qk][r:P:32].bitcast(I32), in_=by_row[r].bitcast(I32))
 
-        load_x(0)
+        for j in range(ROWS):
+            load_x(0, j)
         load_weight(0)
-        load_x(1)
+        for which in range(2):
+            nc.sync.dma_start(out=trig[which][1][:], in_=trig_hbm[which][:, parts[1]])
+        for j in range(ROWS):
+            load_x(1, j)
         load_weight(1)
         for n in range(2, N_GROUPS):
-            load_x(n)
+            for j in range(ROWS):
+                load_x(n, j)
 
         ident = const.tile([P, P], F32)
         make_identity(nc, ident[:])
+        rot = []
+        for at, engine in enumerate((nc.vector, nc.gpsimd)):
+            rot_part = const.tile([P, parts[at].stop - parts[at].start, ROWS, PAIRS, 2, 2], BF16, name="rot%d" % at)
+            rot_v = rot_part[:].rearrange("p s j i e k -> p (s j) i e k")
+            cos_v = trig[0][at][:].rearrange("p s j (i e) -> p (s j) i e", e=2)
+            sin_v = trig[1][at][:].rearrange("p s j (i e) -> p (s j) i e", e=2)
+            engine.tensor_copy(out=rot_v[:, :, :, 0, 0], in_=cos_v[:, :, :, 0])
+            engine.tensor_scalar_mul(out=rot_v[:, :, :, 0, 1], in0=sin_v[:, :, :, 0], scalar1=-1.0)
+            engine.tensor_copy(out=rot_v[:, :, :, 1, 0], in_=sin_v[:, :, :, 1])
+            engine.tensor_copy(out=rot_v[:, :, :, 1, 1], in_=cos_v[:, :, :, 1])
+            rot.append(rot_part)
 
-        rot = const.tile([P, GROUPS_PER_SEQ, ROWS, PAIRS, 2, 2], BF16)
-        rot_v = rot[:].rearrange("p s j i e k -> p (s j) i e k")
-        cos_v = cos_sb[:].rearrange("p s j (i e) -> p (s j) i e", e=2)
-        sin_v = sin_sb[:].rearrange("p s j (i e) -> p (s j) i e", e=2)
-        nc.vector.tensor_copy(out=rot_v[:, :, :, 0, 0], in_=cos_v[:, :, :, 0])
-        nc.vector.tensor_scalar_mul(out=rot_v[:, :, :, 0, 1], in0=sin_v[:, :, :, 0], scalar1=-1.0)
-        nc.vector.tensor_copy(out=rot_v[:, :, :, 1, 0], in_=sin_v[:, :, :, 1])
-        nc.vector.tensor_copy(out=rot_v[:, :, :, 1, 1], in_=cos_v[:, :, :, 1])
+        def rot_of(s, j):
+            return rot[0][:, 0, j] if s == 0 else rot[1][:, s - 1, j]
 
-        def quantise(n):
-            grouped = grouped_pool.tile([P, ROWS, PASSES * P * PACK], BF16, align_bytes=64)
-            for j in range(ROWS):
-                x_words = x_tiles[n][:, j, :].bitcast(F32)
+        def quantise(n, tiles):
+            count = len(tiles)
+            grouped = grouped_pool.tile([P, count, PASSES * P * PACK], BF16, align_bytes=64)
+            for at, j in enumerate(tiles):
+                x_words = x_tiles[n][j][:].bitcast(F32)
                 xt = xt_pool.tile([P, PASSES, 2, P], F32)
                 for g in range(PASSES):
                     for u in range(2):
@@ -104,57 +122,85 @@ def tile_multiscaleretention_pa_t_kernel(
                             ident[:],
                         )
                 nc.scalar.copy(
-                    out=grouped[:, j, :].bitcast(F32).rearrange("p (g r u) -> p g r u", g=PASSES, u=2),
+                    out=grouped[:, at, :].bitcast(F32).rearrange("p (g r u) -> p g r u", g=PASSES, u=2),
                     in_=xt[:].rearrange("p g u r -> p g r u"),
                 )
-            x_codes = mx_pool.tile([P, ROWS, PASSES * P], U32, align_bytes=64)
-            x_planes = mx_pool.tile([P, ROWS, PASSES * P], U8, align_bytes=64)
+            x_codes = mx_pool.tile([P, count, PASSES * P], U32, align_bytes=64)
+            x_planes = mx_pool.tile([P, count, PASSES * P], U8, align_bytes=64)
             nc.vector.quantize_mx(
                 out=x_codes[:].rearrange("p j w -> p (j w)").bitcast(FP8X4),
                 scales=x_planes[:].rearrange("p j w -> p (j w)"),
                 in_=grouped[:].rearrange("p j v -> p (j v)"),
             )
-            return x_codes, x_planes
+            return [(x_codes[:, at, :], x_planes[:, at, :]) for at in range(count)]
 
-        def project(n, qk, x_codes, x_planes):
-            b, s = divmod(n, GROUPS_PER_SEQ)
-            prod = prod_pool.tile([P, ROWS, H, PAIRS, 2, 2], F32)
-            for j in range(ROWS):
-                acc = acc_pool.tile([P, HK], F32)
-                for g in range(PASSES):
-                    tokens = slice(g * P, (g + 1) * P)
-                    nc.tensor.matmul_mx(
-                        out=acc[:],
-                        lhsT=x_codes[:, j, tokens].bitcast(FP8X4),
-                        lhsT_scale=x_planes[:, j, tokens],
-                        rhs=w_words[:, qk, g, :].bitcast(FP8X4),
-                        rhs_scale=w_planes[:, qk, g, :],
-                        start=(g == 0),
-                        stop=(g == PASSES - 1),
-                    )
-                shape = [P, H, PAIRS, 2, 2]
-                nc.vector.tensor_tensor(
-                    out=prod[:, j],
-                    in0=acc[:].rearrange("p (h i k) -> p h i k", h=H, k=2).unsqueeze(3).to_broadcast(shape),
-                    in1=rot[:, s, j].unsqueeze(1).to_broadcast(shape),
-                    op=mybir.AluOpType.mult,
+        def straight(n, qk, j, operand, prod):
+            x_codes, x_planes = operand
+            acc = acc_pool.tile([P, HK], F32)
+            for g in range(PASSES):
+                tokens = slice(g * P, (g + 1) * P)
+                nc.tensor.matmul_mx(
+                    out=acc[:],
+                    lhsT=x_codes[:, tokens].bitcast(FP8X4),
+                    lhsT_scale=x_planes[:, tokens],
+                    rhs=w_words[qk][:, g, :].bitcast(FP8X4),
+                    rhs_scale=w_planes[qk][:, g, :],
+                    start=(g == 0),
+                    stop=(g == PASSES - 1),
                 )
-            stage = stage_pool.tile([P, H, ROWS, DK], F32)
-            terms = prod[:].rearrange("p j h i e k -> p j h (i e) k")
-            nc.gpsimd.tensor_tensor(
-                out=stage[:].rearrange("p h j c -> p j h c"),
-                in0=terms[:, :, :, :, 0],
-                in1=terms[:, :, :, :, 1],
-                op=mybir.AluOpType.add,
+            shape = [P, H, PAIRS, 2, 2]
+            nc.vector.tensor_tensor(
+                out=prod[:, j],
+                in0=acc[:].rearrange("p (h i k) -> p h i k", h=H, k=2).unsqueeze(3).to_broadcast(shape),
+                in1=rot_of(n % GROUPS_PER_SEQ, j).unsqueeze(1).to_broadcast(shape),
+                op=MULT,
             )
+
+        def add_up(engine, prod, stage, rows):
+            terms = prod[:].rearrange("p j h i e k -> p j h (i e) k")
+            engine.tensor_tensor(
+                out=stage[:].rearrange("p h j c -> p j h c")[:, rows],
+                in0=terms[:, rows, :, :, 0],
+                in1=terms[:, rows, :, :, 1],
+                op=ADD,
+            )
+
+        def store(n, qk, stage):
+            b, s = divmod(n, GROUPS_PER_SEQ)
             nc.sync.dma_start(
                 out=outs[qk][b].rearrange("h (s p j) c -> s p h (j c)", p=P, j=ROWS)[s],
                 in_=stage[:].rearrange("p h j c -> p h (j c)"),
             )
 
-        ready = quantise(0)
-        for n in range(N_GROUPS):
-            project(n, 0, ready[0], ready[1])
-            following = quantise(n + 1) if n + 1 < N_GROUPS else None
-            project(n, 1, ready[0], ready[1])
+        def store_row(n, qk, j, stage):
+            b, s = divmod(n, GROUPS_PER_SEQ)
+            nc.sync.dma_start(
+                out=outs[qk][b].rearrange("h (s p j) c -> s j p h c", p=P, j=ROWS)[s][j],
+                in_=stage[:, :, j, :],
+            )
+
+        def project(n, qk, operands):
+            prod = prod_pool.tile([P, ROWS, H, PAIRS, 2, 2], F32)
+            stage = stage_pool.tile([P, H, ROWS, DK], F32)
+            if n < N_GROUPS - 1:
+                for j in range(ROWS):
+                    straight(n, qk, j, operands[j], prod)
+                add_up(nc.gpsimd, prod, stage, slice(0, ROWS))
+                store(n, qk, stage)
+                return
+            for j in range(ROWS):
+                straight(n, qk, j, operands[j], prod)
+                engine = nc.vector if (qk, j) == (1, ROWS - 1) else nc.gpsimd
+                add_up(engine, prod, stage, slice(j, j + 1))
+                store_row(n, qk, j, stage)
+
+        with tc.manual_schedule(engines={mybir.EngineType.PE}):
+            ready = quantise(0, [0]) + quantise(0, [1])
+            project(0, 0, ready)
+            following = quantise(1, list(range(ROWS)))
+        project(0, 1, ready)
+        for n in range(1, N_GROUPS):
             ready = following
+            project(n, 0, ready)
+            following = quantise(n + 1, list(range(ROWS))) if n + 1 < N_GROUPS else None
+            project(n, 1, ready)

@@ -41,10 +41,10 @@ def tile_multiscaleretention_pa_t_kernel(
     with ExitStack() as ctx:
         const = ctx.enter_context(tc.tile_pool(name="const", bufs=1))
         x_pool = ctx.enter_context(tc.tile_pool(name="x", bufs=N_GROUPS * ROWS))
-        grouped_pool = ctx.enter_context(tc.tile_pool(name="grouped", bufs=2))
-        mx_pool = ctx.enter_context(tc.tile_pool(name="mx", bufs=4))
-        prod_pool = ctx.enter_context(tc.tile_pool(name="prod", bufs=5))
-        stage_pool = ctx.enter_context(tc.tile_pool(name="stage", bufs=12))
+        grouped_pool = ctx.enter_context(tc.tile_pool(name="grouped", bufs=3))
+        mx_pool = ctx.enter_context(tc.tile_pool(name="mx", bufs=5))
+        prod_pool = ctx.enter_context(tc.tile_pool(name="prod", bufs=3))
+        stage_pool = ctx.enter_context(tc.tile_pool(name="stage", bufs=6))
         xt_pool = ctx.enter_context(tc.psum_pool(name="xt", bufs=ROWS))
         acc_pool = ctx.enter_context(tc.psum_pool(name="acc", bufs=8 - ROWS))
 
@@ -150,57 +150,72 @@ def tile_multiscaleretention_pa_t_kernel(
                 )
             shape = [P, H, PAIRS, 2, 2]
             nc.vector.tensor_tensor(
-                out=prod[:, j],
+                out=prod[:, qk, :, j],
                 in0=acc[:].rearrange("p (h i k) -> p h i k", h=H, k=2).unsqueeze(3).to_broadcast(shape),
                 in1=rot_of(n % GROUPS_PER_SEQ, j).unsqueeze(1).to_broadcast(shape),
                 op=MULT,
             )
 
-        def add_up(engine, prod, stage, rows):
-            terms = prod[:].rearrange("p j h i e k -> p j h (i e) k")
-            engine.tensor_tensor(
-                out=stage[:].rearrange("p h j c -> p j h c")[:, rows],
-                in0=terms[:, rows, :, :, 0],
-                in1=terms[:, rows, :, :, 1],
+        def add_up(prod, stage, first, count):
+            terms = prod[:, first : first + count].rearrange("p q h j i e k -> p (q h j i e) k")
+            nc.gpsimd.tensor_tensor(
+                out=stage[:, first : first + count].rearrange("p q h j c -> p (q h j c)"),
+                in0=terms[:, :, 0],
+                in1=terms[:, :, 1],
                 op=ADD,
             )
+
+        def add_up_row(engine, prod, stage, qk, j):
+            terms = prod[:, qk, :, j].rearrange("p h i e k -> p h (i e) k")
+            engine.tensor_tensor(out=stage[:, qk, :, j, :], in0=terms[:, :, :, 0], in1=terms[:, :, :, 1], op=ADD)
 
         def store(n, qk, stage):
             b, s = divmod(n, GROUPS_PER_SEQ)
             nc.sync.dma_start(
                 out=outs[qk][b].rearrange("h (s p j) c -> s p h (j c)", p=P, j=ROWS)[s],
-                in_=stage[:].rearrange("p h j c -> p h (j c)"),
+                in_=stage[:, qk].rearrange("p h j c -> p h (j c)"),
             )
 
         def store_row(n, qk, j, stage):
             b, s = divmod(n, GROUPS_PER_SEQ)
             nc.sync.dma_start(
                 out=outs[qk][b].rearrange("h (s p j) c -> s j p h c", p=P, j=ROWS)[s][j],
-                in_=stage[:, :, j, :],
+                in_=stage[:, qk, :, j, :],
             )
 
-        def project(n, qk, operands):
-            prod = prod_pool.tile([P, ROWS, H, PAIRS, 2, 2], F32)
-            stage = stage_pool.tile([P, H, ROWS, DK], F32)
-            if n < N_GROUPS - 1:
-                for j in range(ROWS):
-                    straight(n, qk, j, operands[j], prod)
-                add_up(nc.gpsimd, prod, stage, slice(0, ROWS))
-                store(n, qk, stage)
-                return
-            for j in range(ROWS):
-                straight(n, qk, j, operands[j], prod)
-                engine = nc.vector if (qk, j) == (1, ROWS - 1) else nc.gpsimd
-                add_up(engine, prod, stage, slice(j, j + 1))
-                store_row(n, qk, j, stage)
+        whole = list(range(ROWS))
+        codes = {}
+        tiles = {}
 
-        with tc.manual_schedule(engines={mybir.EngineType.PE}):
-            ready = quantise(0, [0]) + quantise(0, [1])
-            project(0, 0, ready)
-            following = quantise(1, list(range(ROWS)))
-        project(0, 1, ready)
-        for n in range(1, N_GROUPS):
-            ready = following
-            project(n, 0, ready)
-            following = quantise(n + 1, list(range(ROWS))) if n + 1 < N_GROUPS else None
-            project(n, 1, ready)
+        def products(n, qk):
+            if qk == 0:
+                prod = prod_pool.tile([P, 2, H, ROWS, PAIRS, 2, 2], F32)
+                stage = stage_pool.tile([P, 2, H, ROWS, DK], F32)
+                tiles[n] = (prod, stage)
+            prod, stage = tiles[n]
+            for j in range(ROWS):
+                straight(n, qk, j, codes[n][j], prod)
+            if n == 0 or n == N_GROUPS - 2:
+                add_up(prod, stage, qk, 1)
+                store(n, qk, stage)
+
+        with tc.manual_schedule(engines={mybir.EngineType.PE, mybir.EngineType.DVE}):
+            codes[0] = quantise(0, [0]) + quantise(0, [1])
+            products(0, 0)
+            codes[1] = quantise(1, whole)
+        with tc.manual_schedule(engines={mybir.EngineType.DVE}):
+            for n in range(N_GROUPS):
+                if n > 0:
+                    products(n, 0)
+                products(n, 1)
+                if 0 < n < N_GROUPS - 2:
+                    add_up(tiles[n][0], tiles[n][1], 0, 2)
+                    for qk in range(2):
+                        store(n, qk, tiles[n][1])
+                if n + 2 < N_GROUPS:
+                    codes[n + 2] = quantise(n + 2, whole)
+            for qk in range(2):
+                for j in range(ROWS):
+                    engine = nc.gpsimd if (qk, j) == (0, 0) else nc.vector
+                    add_up_row(engine, tiles[N_GROUPS - 1][0], tiles[N_GROUPS - 1][1], qk, j)
+                    store_row(N_GROUPS - 1, qk, j, tiles[N_GROUPS - 1][1])

@@ -25,6 +25,7 @@ WORDS = K_PASS // 2
 ROWS = 2
 GROUPS_PER_SEQ = T // (P * ROWS)
 N_GROUPS = B * GROUPS_PER_SEQ
+PE_HEADS = 2
 
 FLOPS = 2 * B * T * E * 2 * HK
 
@@ -41,12 +42,15 @@ def tile_multiscaleretention_pa_t_kernel(
     with ExitStack() as ctx:
         const = ctx.enter_context(tc.tile_pool(name="const", bufs=1))
         x_pool = ctx.enter_context(tc.tile_pool(name="x", bufs=N_GROUPS * ROWS))
-        grouped_pool = ctx.enter_context(tc.tile_pool(name="grouped", bufs=3))
+        grouped_pool = ctx.enter_context(tc.tile_pool(name="grouped", bufs=2))
         mx_pool = ctx.enter_context(tc.tile_pool(name="mx", bufs=5))
         prod_pool = ctx.enter_context(tc.tile_pool(name="prod", bufs=3))
-        stage_pool = ctx.enter_context(tc.tile_pool(name="stage", bufs=6))
+        stage_pool = ctx.enter_context(tc.tile_pool(name="stage", bufs=7))
         xt_pool = ctx.enter_context(tc.psum_pool(name="xt", bufs=ROWS))
-        acc_pool = ctx.enter_context(tc.psum_pool(name="acc", bufs=8 - ROWS))
+        acc_pool = ctx.enter_context(tc.psum_pool(name="acc", bufs=4))
+        sum_t_pool = ctx.enter_context(tc.psum_pool(name="sum_t", bufs=1))
+        sum_pool = ctx.enter_context(tc.psum_pool(name="sum", bufs=1))
+        turned_pool = ctx.enter_context(tc.tile_pool(name="turned", bufs=2))
 
         parts = (slice(0, 1), slice(1, GROUPS_PER_SEQ))
         trig = [
@@ -165,6 +169,39 @@ def tile_multiscaleretention_pa_t_kernel(
                 op=ADD,
             )
 
+        def add_up_most(prod, stage):
+            count = (2 * H - PE_HEADS) * ROWS * DK
+            terms = prod[:].rearrange("p q h j i e k -> p (q h j i e) k")
+            nc.gpsimd.tensor_tensor(
+                out=stage[:].rearrange("p q h j c -> p (q h j c)")[:, :count],
+                in0=terms[:, :count, 0],
+                in1=terms[:, :count, 1],
+                op=ADD,
+            )
+
+        def sum_turned(prod):
+            sum_t = sum_t_pool.tile([P, PE_HEADS, P], F32)
+            for at in range(PE_HEADS):
+                terms = prod[:, 1, H - PE_HEADS + at].rearrange("p j i e k -> p (j i e) k")
+                for k in range(2):
+                    nc.tensor.matmul(
+                        sum_t[:, at, :],
+                        lhsT=terms[:, :, k],
+                        rhs=ident[:],
+                        is_transpose=True,
+                        start=(k == 0),
+                        stop=(k == 1),
+                    )
+            turned = turned_pool.tile([P, PE_HEADS, P], F32)
+            nc.scalar.copy(out=turned[:], in_=sum_t[:])
+            return turned
+
+        def turn_back(turned, stage):
+            total = sum_pool.tile([P, PE_HEADS, P], F32)
+            for at in range(PE_HEADS):
+                nc.tensor.transpose(total[:, at, :], turned[:, at, :], ident[:])
+            nc.scalar.copy(out=stage[:, 1, H - PE_HEADS :].rearrange("p h j c -> p h (j c)"), in_=total[:])
+
         def add_up_row(engine, prod, stage, qk, j):
             terms = prod[:, qk, :, j].rearrange("p h i e k -> p h (i e) k")
             engine.tensor_tensor(out=stage[:, qk, :, j, :], in0=terms[:, :, :, 0], in1=terms[:, :, :, 1], op=ADD)
@@ -186,6 +223,7 @@ def tile_multiscaleretention_pa_t_kernel(
         whole = list(range(ROWS))
         codes = {}
         tiles = {}
+        turned_sums = {}
 
         def products(n, qk):
             if qk == 0:
@@ -209,9 +247,13 @@ def tile_multiscaleretention_pa_t_kernel(
                     products(n, 0)
                 products(n, 1)
                 if 0 < n < N_GROUPS - 2:
-                    add_up(tiles[n][0], tiles[n][1], 0, 2)
-                    for qk in range(2):
-                        store(n, qk, tiles[n][1])
+                    add_up_most(tiles[n][0], tiles[n][1])
+                    store(n, 0, tiles[n][1])
+                if n - 2 in turned_sums:
+                    turn_back(turned_sums[n - 2], tiles[n - 2][1])
+                    store(n - 2, 1, tiles[n - 2][1])
+                if 0 < n - 1 < N_GROUPS - 2:
+                    turned_sums[n - 1] = sum_turned(tiles[n - 1][0])
                 if n + 2 < N_GROUPS:
                     codes[n + 2] = quantise(n + 2, whole)
             for qk in range(2):

@@ -103,10 +103,13 @@ def tile_multiscaleretention_pa_t_kernel(
             rot_v = rot_part[:].rearrange("p s j i e k -> p (s j) i e k")
             cos_v = trig[0][at][:].rearrange("p s j (i e) -> p (s j) i e", e=2)
             sin_v = trig[1][at][:].rearrange("p s j (i e) -> p (s j) i e", e=2)
-            engine.tensor_copy(out=rot_v[:, :, :, 0, 0], in_=cos_v[:, :, :, 0])
-            engine.tensor_scalar_mul(out=rot_v[:, :, :, 0, 1], in0=sin_v[:, :, :, 0], scalar1=-1.0)
-            engine.tensor_copy(out=rot_v[:, :, :, 1, 0], in_=sin_v[:, :, :, 1])
-            engine.tensor_copy(out=rot_v[:, :, :, 1, 1], in_=cos_v[:, :, :, 1])
+            flat_v = rot_v.rearrange("p s i e k -> p s i (e k)")
+            for out, in_, sign in (
+                (flat_v[:, :, :, 0::3], cos_v, 1.0),
+                (flat_v[:, :, :, 1], sin_v[:, :, :, 0], -1.0),
+                (flat_v[:, :, :, 2], sin_v[:, :, :, 1], 1.0),
+            ):
+                engine.tensor_scalar(out=out, in0=in_, scalar1=sign, scalar2=0.0, op0=MULT, op1=ADD)
             rot.append(rot_part)
 
         def rot_of(s, j):
@@ -138,8 +141,8 @@ def tile_multiscaleretention_pa_t_kernel(
             )
             return [(x_codes[:, at, :], x_planes[:, at, :]) for at in range(count)]
 
-        def straight(n, qk, j, operand, prod):
-            x_codes, x_planes = operand
+        def project(n, qk, j):
+            x_codes, x_planes = codes[n][j]
             acc = acc_pool.tile([P, HK], F32)
             for g in range(PASSES):
                 tokens = slice(g * P, (g + 1) * P)
@@ -152,17 +155,21 @@ def tile_multiscaleretention_pa_t_kernel(
                     start=(g == 0),
                     stop=(g == PASSES - 1),
                 )
-            shape = [P, H, PAIRS, 2, 2]
+            return acc
+
+        def multiply(n, qk, j, acc, prod, heads=slice(0, H)):
+            shape = [P, heads.stop - heads.start, PAIRS, 2, 2]
+            u = acc[:].rearrange("p (h i k) -> p h i k", h=H, k=2)[:, heads]
             nc.vector.tensor_tensor(
-                out=prod[:, qk, :, j],
-                in0=acc[:].rearrange("p (h i k) -> p h i k", h=H, k=2).unsqueeze(3).to_broadcast(shape),
+                out=prod[:, qk, heads, j],
+                in0=u.unsqueeze(3).to_broadcast(shape),
                 in1=rot_of(n % GROUPS_PER_SEQ, j).unsqueeze(1).to_broadcast(shape),
                 op=MULT,
             )
 
-        def add_up(prod, stage, first, count):
+        def add_up(engine, prod, stage, first, count):
             terms = prod[:, first : first + count].rearrange("p q h j i e k -> p (q h j i e) k")
-            nc.gpsimd.tensor_tensor(
+            engine.tensor_tensor(
                 out=stage[:, first : first + count].rearrange("p q h j c -> p (q h j c)"),
                 in0=terms[:, :, 0],
                 in1=terms[:, :, 1],
@@ -202,10 +209,6 @@ def tile_multiscaleretention_pa_t_kernel(
                 nc.tensor.transpose(total[:, at, :], turned[:, at, :], ident[:])
             nc.scalar.copy(out=stage[:, 1, H - PE_HEADS :].rearrange("p h j c -> p h (j c)"), in_=total[:])
 
-        def add_up_row(engine, prod, stage, qk, j):
-            terms = prod[:, qk, :, j].rearrange("p h i e k -> p h (i e) k")
-            engine.tensor_tensor(out=stage[:, qk, :, j, :], in0=terms[:, :, :, 0], in1=terms[:, :, :, 1], op=ADD)
-
         def store(n, qk, stage):
             b, s = divmod(n, GROUPS_PER_SEQ)
             nc.sync.dma_start(
@@ -213,17 +216,11 @@ def tile_multiscaleretention_pa_t_kernel(
                 in_=stage[:, qk].rearrange("p h j c -> p h (j c)"),
             )
 
-        def store_row(n, qk, j, stage):
-            b, s = divmod(n, GROUPS_PER_SEQ)
-            nc.sync.dma_start(
-                out=outs[qk][b].rearrange("h (s p j) c -> s j p h c", p=P, j=ROWS)[s][j],
-                in_=stage[:, qk, :, j, :],
-            )
-
         whole = list(range(ROWS))
         codes = {}
         tiles = {}
         turned_sums = {}
+        gate = []
 
         def products(n, qk):
             if qk == 0:
@@ -232,9 +229,14 @@ def tile_multiscaleretention_pa_t_kernel(
                 tiles[n] = (prod, stage)
             prod, stage = tiles[n]
             for j in range(ROWS):
-                straight(n, qk, j, codes[n][j], prod)
-            if n == 0 or n == N_GROUPS - 2:
-                add_up(prod, stage, qk, 1)
+                acc = project(n, qk, j)
+                if (n, qk, j) == (0, 1, ROWS - 1):
+                    multiply(n, qk, j, acc, prod, slice(1, H))
+                    gate.append(lambda: multiply(n, qk, j, acc, prod, slice(0, 1)))
+                else:
+                    multiply(n, qk, j, acc, prod)
+            if n == N_GROUPS - 2:
+                add_up(nc.gpsimd, prod, stage, qk, 1)
                 store(n, qk, stage)
 
         with tc.manual_schedule(engines={mybir.EngineType.PE, mybir.EngineType.DVE}):
@@ -246,18 +248,20 @@ def tile_multiscaleretention_pa_t_kernel(
                 if n > 0:
                     products(n, 0)
                 products(n, 1)
-                if 0 < n < N_GROUPS - 2:
+                if n == 0:
+                    codes[2] = quantise(2, whole)
+                    gate[0]()
+                if n < N_GROUPS - 2:
                     add_up_most(tiles[n][0], tiles[n][1])
                     store(n, 0, tiles[n][1])
                 if n - 2 in turned_sums:
                     turn_back(turned_sums[n - 2], tiles[n - 2][1])
                     store(n - 2, 1, tiles[n - 2][1])
-                if 0 < n - 1 < N_GROUPS - 2:
+                if 0 <= n - 1 < N_GROUPS - 2:
                     turned_sums[n - 1] = sum_turned(tiles[n - 1][0])
-                if n + 2 < N_GROUPS:
+                if 0 < n and n + 2 < N_GROUPS:
                     codes[n + 2] = quantise(n + 2, whole)
+            prod, stage = tiles[N_GROUPS - 1]
             for qk in range(2):
-                for j in range(ROWS):
-                    engine = nc.gpsimd if (qk, j) == (0, 0) else nc.vector
-                    add_up_row(engine, tiles[N_GROUPS - 1][0], tiles[N_GROUPS - 1][1], qk, j)
-                    store_row(N_GROUPS - 1, qk, j, tiles[N_GROUPS - 1][1])
+                add_up(nc.vector, prod, stage, qk, 1)
+                store(N_GROUPS - 1, qk, stage)

from contextlib import ExitStack

import concourse.mybir as mybir
from concourse.masks import make_identity

F32 = mybir.dt.float32
BF16 = mybir.dt.bfloat16
I32 = mybir.dt.int32
U32 = mybir.dt.uint32
U8 = mybir.dt.uint8
FP8X4 = mybir.dt.float8_e4m3fn_x4
MULT = mybir.AluOpType.mult
ADD = mybir.AluOpType.add

B, T, H, DK, E = 4, 1024, 8, 64, 1024
HK = H * DK
PAIRS = DK // 2

P = 128
PACK = 4
K_PASS = P * PACK
PASSES = E // K_PASS
WORDS = K_PASS // 2

ROWS = 2
GROUPS_PER_SEQ = T // (P * ROWS)
N_GROUPS = B * GROUPS_PER_SEQ
PE_HEADS = 2

FLOPS = 2 * B * T * E * 2 * HK


def tile_multiscaleretention_pa_t_kernel(
    tc, x, sin, cos, Wq_words, Wq_scales, Wk_words, Wk_scales, out_0, out_1
):
    nc = tc.nc
    weights = ((Wq_words, Wq_scales), (Wk_words, Wk_scales))
    outs = (out_0, out_1)
    x_groups = x.rearrange("b (s p j) e -> (b s) p j e", p=P, j=ROWS)
    trig_hbm = [t.rearrange("(s p j) c -> p s j c", p=P, j=ROWS) for t in (cos, sin)]

    with ExitStack() as ctx:
        const = ctx.enter_context(tc.tile_pool(name="const", bufs=1))
        x_pool = ctx.enter_context(tc.tile_pool(name="x", bufs=N_GROUPS * ROWS))
        grouped_pool = ctx.enter_context(tc.tile_pool(name="grouped", bufs=2))
        mx_pool = ctx.enter_context(tc.tile_pool(name="mx", bufs=5))
        prod_pool = ctx.enter_context(tc.tile_pool(name="prod", bufs=3))
        stage_pool = ctx.enter_context(tc.tile_pool(name="stage", bufs=7))
        xt_pool = ctx.enter_context(tc.psum_pool(name="xt", bufs=ROWS))
        acc_pool = ctx.enter_context(tc.psum_pool(name="acc", bufs=4))
        sum_t_pool = ctx.enter_context(tc.psum_pool(name="sum_t", bufs=1))
        sum_pool = ctx.enter_context(tc.psum_pool(name="sum", bufs=1))
        turned_pool = ctx.enter_context(tc.tile_pool(name="turned", bufs=2))

        parts = (slice(0, 1), slice(1, GROUPS_PER_SEQ))
        trig = [
            [
                const.tile([P, part.stop - part.start, ROWS, DK], BF16, name="trig%d%d" % (which, at))
                for at, part in enumerate(parts)
            ]
            for which in range(2)
        ]
        for which in range(2):
            nc.scalar.dma_start(out=trig[which][0][:], in_=trig_hbm[which][:, parts[0]])

        w_words = [const.tile([P, PASSES, HK], U32, align_bytes=64, name="w_words%d" % qk) for qk in range(2)]
        w_planes = [const.tile([P, PASSES, HK], U8, align_bytes=64, name="w_planes%d" % qk) for qk in range(2)]
        for qk in range(2):
            nc.vector.memset(w_planes[qk][:].bitcast(I32), 0)

        x_tiles = [[x_pool.tile([P, E], BF16, name="x_sb") for j in range(ROWS)] for n in range(N_GROUPS)]

        def load_x(n, j):
            nc.sync.dma_start(out=x_tiles[n][j][:], in_=x_groups[n][:, j, :])

        def load_weight(qk):
            words, scales = weights[qk]
            nc.sync.dma_start(
                out=w_words[qk][:].bitcast(I32),
                in_=words.rearrange("g p n t -> p g (n t)").bitcast(I32),
            )
            by_row = scales.rearrange("g (q r) n -> r q g n", r=4)
            for r in range(4):
                nc.sync.dma_start(out=w_planes[qk][r:P:32].bitcast(I32), in_=by_row[r].bitcast(I32))

        for j in range(ROWS):
            load_x(0, j)
        load_weight(0)
        for which in range(2):
            nc.sync.dma_start(out=trig[which][1][:], in_=trig_hbm[which][:, parts[1]])
        for j in range(ROWS):
            load_x(1, j)
        load_weight(1)
        for n in range(2, N_GROUPS):
            for j in range(ROWS):
                load_x(n, j)

        ident = const.tile([P, P], F32)
        make_identity(nc, ident[:])
        rot = []
        for at, engine in enumerate((nc.vector, nc.gpsimd)):
            rot_part = const.tile([P, parts[at].stop - parts[at].start, ROWS, PAIRS, 2, 2], BF16, name="rot%d" % at)
            rot_v = rot_part[:].rearrange("p s j i e k -> p (s j) i e k")
            cos_v = trig[0][at][:].rearrange("p s j (i e) -> p (s j) i e", e=2)
            sin_v = trig[1][at][:].rearrange("p s j (i e) -> p (s j) i e", e=2)
            flat_v = rot_v.rearrange("p s i e k -> p s i (e k)")
            for out, in_, sign in (
                (flat_v[:, :, :, 0::3], cos_v, 1.0),
                (flat_v[:, :, :, 1], sin_v[:, :, :, 0], -1.0),
                (flat_v[:, :, :, 2], sin_v[:, :, :, 1], 1.0),
            ):
                engine.tensor_scalar(out=out, in0=in_, scalar1=sign, scalar2=0.0, op0=MULT, op1=ADD)
            rot.append(rot_part)

        def rot_of(s, j):
            return rot[0][:, 0, j] if s == 0 else rot[1][:, s - 1, j]

        def quantise(n, tiles):
            count = len(tiles)
            grouped = grouped_pool.tile([P, count, PASSES * P * PACK], BF16, align_bytes=64)
            for at, j in enumerate(tiles):
                x_words = x_tiles[n][j][:].bitcast(F32)
                xt = xt_pool.tile([P, PASSES, 2, P], F32)
                for g in range(PASSES):
                    for u in range(2):
                        nc.tensor.transpose(
                            xt[:, g, u, :],
                            x_words[:, WORDS * g + u : WORDS * (g + 1) : 2],
                            ident[:],
                        )
                nc.scalar.copy(
                    out=grouped[:, at, :].bitcast(F32).rearrange("p (g r u) -> p g r u", g=PASSES, u=2),
                    in_=xt[:].rearrange("p g u r -> p g r u"),
                )
            x_codes = mx_pool.tile([P, count, PASSES * P], U32, align_bytes=64)
            x_planes = mx_pool.tile([P, count, PASSES * P], U8, align_bytes=64)
            nc.vector.quantize_mx(
                out=x_codes[:].rearrange("p j w -> p (j w)").bitcast(FP8X4),
                scales=x_planes[:].rearrange("p j w -> p (j w)"),
                in_=grouped[:].rearrange("p j v -> p (j v)"),
            )
            return [(x_codes[:, at, :], x_planes[:, at, :]) for at in range(count)]

        def project(n, qk, j):
            x_codes, x_planes = codes[n][j]
            acc = acc_pool.tile([P, HK], F32)
            for g in range(PASSES):
                tokens = slice(g * P, (g + 1) * P)
                nc.tensor.matmul_mx(
                    out=acc[:],
                    lhsT=x_codes[:, tokens].bitcast(FP8X4),
                    lhsT_scale=x_planes[:, tokens],
                    rhs=w_words[qk][:, g, :].bitcast(FP8X4),
                    rhs_scale=w_planes[qk][:, g, :],
                    start=(g == 0),
                    stop=(g == PASSES - 1),
                )
            return acc

        def multiply(n, qk, j, acc, prod, heads=slice(0, H)):
            shape = [P, heads.stop - heads.start, PAIRS, 2, 2]
            u = acc[:].rearrange("p (h i k) -> p h i k", h=H, k=2)[:, heads]
            nc.vector.tensor_tensor(
                out=prod[:, qk, heads, j],
                in0=u.unsqueeze(3).to_broadcast(shape),
                in1=rot_of(n % GROUPS_PER_SEQ, j).unsqueeze(1).to_broadcast(shape),
                op=MULT,
            )

        def add_up(engine, prod, stage, first, count):
            terms = prod[:, first : first + count].rearrange("p q h j i e k -> p (q h j i e) k")
            engine.tensor_tensor(
                out=stage[:, first : first + count].rearrange("p q h j c -> p (q h j c)"),
                in0=terms[:, :, 0],
                in1=terms[:, :, 1],
                op=ADD,
            )

        def add_up_most(prod, stage):
            count = (2 * H - PE_HEADS) * ROWS * DK
            terms = prod[:].rearrange("p q h j i e k -> p (q h j i e) k")
            nc.gpsimd.tensor_tensor(
                out=stage[:].rearrange("p q h j c -> p (q h j c)")[:, :count],
                in0=terms[:, :count, 0],
                in1=terms[:, :count, 1],
                op=ADD,
            )

        def sum_turned(prod):
            sum_t = sum_t_pool.tile([P, PE_HEADS, P], F32)
            for at in range(PE_HEADS):
                terms = prod[:, 1, H - PE_HEADS + at].rearrange("p j i e k -> p (j i e) k")
                for k in range(2):
                    nc.tensor.matmul(
                        sum_t[:, at, :],
                        lhsT=terms[:, :, k],
                        rhs=ident[:],
                        is_transpose=True,
                        start=(k == 0),
                        stop=(k == 1),
                    )
            turned = turned_pool.tile([P, PE_HEADS, P], F32)
            nc.scalar.copy(out=turned[:], in_=sum_t[:])
            return turned

        def turn_back(turned, stage):
            total = sum_pool.tile([P, PE_HEADS, P], F32)
            for at in range(PE_HEADS):
                nc.tensor.transpose(total[:, at, :], turned[:, at, :], ident[:])
            nc.scalar.copy(out=stage[:, 1, H - PE_HEADS :].rearrange("p h j c -> p h (j c)"), in_=total[:])

        def store(n, qk, stage):
            b, s = divmod(n, GROUPS_PER_SEQ)
            nc.sync.dma_start(
                out=outs[qk][b].rearrange("h (s p j) c -> s p h (j c)", p=P, j=ROWS)[s],
                in_=stage[:, qk].rearrange("p h j c -> p h (j c)"),
            )

        whole = list(range(ROWS))
        codes = {}
        tiles = {}
        turned_sums = {}
        gate = []

        def products(n, qk):
            if qk == 0:
                prod = prod_pool.tile([P, 2, H, ROWS, PAIRS, 2, 2], F32)
                stage = stage_pool.tile([P, 2, H, ROWS, DK], F32)
                tiles[n] = (prod, stage)
            prod, stage = tiles[n]
            for j in range(ROWS):
                acc = project(n, qk, j)
                if (n, qk, j) == (0, 1, ROWS - 1):
                    multiply(n, qk, j, acc, prod, slice(1, H))
                    gate.append(lambda: multiply(n, qk, j, acc, prod, slice(0, 1)))
                else:
                    multiply(n, qk, j, acc, prod)
            if n == N_GROUPS - 2:
                add_up(nc.gpsimd, prod, stage, qk, 1)
                store(n, qk, stage)

        with tc.manual_schedule(engines={mybir.EngineType.PE, mybir.EngineType.DVE}):
            codes[0] = quantise(0, [0]) + quantise(0, [1])
            products(0, 0)
            codes[1] = quantise(1, whole)
        with tc.manual_schedule(engines={mybir.EngineType.DVE}):
            for n in range(N_GROUPS):
                if n > 0:
                    products(n, 0)
                products(n, 1)
                if n == 0:
                    codes[2] = quantise(2, whole)
                    gate[0]()
                if n < N_GROUPS - 2:
                    add_up_most(tiles[n][0], tiles[n][1])
                    store(n, 0, tiles[n][1])
                if n - 2 in turned_sums:
                    turn_back(turned_sums[n - 2], tiles[n - 2][1])
                    store(n - 2, 1, tiles[n - 2][1])
                if 0 <= n - 1 < N_GROUPS - 2:
                    turned_sums[n - 1] = sum_turned(tiles[n - 1][0])
                if 0 < n and n + 2 < N_GROUPS:
                    codes[n + 2] = quantise(n + 2, whole)
            prod, stage = tiles[N_GROUPS - 1]
            for qk in range(2):
                add_up(nc.vector, prod, stage, qk, 1)
                store(N_GROUPS - 1, qk, stage)
